import numpy as np
import ml_dtypes


def mxq(x, axis, fmt="e4m3"):
    dtype, down = {"e4m3": (ml_dtypes.float8_e4m3fn, 7), "e5m2": (ml_dtypes.float8_e5m2, 14)}[fmt]
    v = np.moveaxis(np.asarray(x, np.float32).astype(ml_dtypes.bfloat16).astype(np.float64), axis, -1)
    blocks = v.reshape(v.shape[:-1] + (-1, 32))
    amax = np.abs(blocks).max(-1, keepdims=True)
    byte = np.maximum(np.where(amax > 0, np.frexp(amax)[1] - 1 + 127, 0) - down, 1)
    scale = np.exp2(byte - 127.0)
    codes = (blocks / scale).astype(np.float32).astype(dtype).astype(np.float64)
    return np.moveaxis((codes * scale).reshape(v.shape), -1, axis)


WIDE = False


def mx_kscale(k):
    if not WIDE:
        return np.ones(k)
    levels = np.array([10, -10, 5, -5, 0])
    a = np.random.permutation(np.resize(levels, k // 512 * 4)).reshape(k // 512, 4)
    idx = np.arange(k)
    return np.exp2(a[idx // 512, idx % 128 // 32])


BF16 = ml_dtypes.bfloat16


def bf(x):
    return np.asarray(x, np.float32).astype(BF16)


def f64(x):
    return np.asarray(x).astype(np.float64)


E2M1 = np.array([0.0, 0.5, 1.0, 1.5, 2.0, 3.0, 4.0, 6.0, -0.0, -0.5, -1.0, -1.5, -2.0, -3.0, -4.0, -6.0])


def pack_weight(w, fmt):
    k, n = w.shape
    w = f64(bf(w)).reshape(k // 32, 32, n)
    amax = np.abs(w).max(1)
    if fmt == "e4m3":
        byte = np.frexp(amax)[1] - 1 + 127 - 7
    else:
        mant, ex = np.frexp(amax / 6.0)
        byte = np.where(mant > 0.5, ex, ex - 1) + 127
    byte = np.clip(np.where(amax > 0, byte, 1), 1, 254)
    scaled = (w * np.exp2(127.0 - byte)[:, None, :]).reshape(k, n).astype(np.float32)
    by_word = np.ascontiguousarray(scaled.reshape(k // 512, 128, 4, n).transpose(0, 1, 3, 2))
    if fmt == "e4m3":
        words = by_word.astype(ml_dtypes.float8_e4m3fn).view(np.uint8)
    else:
        c = by_word.astype(ml_dtypes.float4_e2m1fn).view(np.uint8) & 0xF
        words = c[..., 0::2] | (c[..., 1::2] << 4)
    return np.ascontiguousarray(words), np.ascontiguousarray(byte.astype(np.uint8).reshape(k // 512, 16, n))


def unpack_weight(words, scales, fmt):
    g, p, n, _ = words.shape
    if fmt == "e4m3":
        vals = np.ascontiguousarray(words).view(ml_dtypes.float8_e4m3fn).astype(np.float64)
    else:
        nib = np.empty((g, p, n, 4), np.uint8)
        nib[..., 0::2] = words & 0xF
        nib[..., 1::2] = words >> 4
        vals = E2M1[nib]
    vals = vals * np.repeat(np.exp2(scales.astype(np.float64) - 127.0), 8, axis=1)[..., None]
    return vals.transpose(0, 1, 3, 2).reshape(g * 512, n)


B, I, U = 128, 2048, 2048


def sigmoid(v):
    return 1.0 / (1.0 + np.exp(-v))


def setup_inputs():
    s = mx_kscale(I)
    x_t = bf(np.random.standard_normal((B, I)) * s)
    h_tm1 = bf(np.random.standard_normal((B, U)))
    iw_words, iw_scales = pack_weight(np.random.standard_normal((I, U * 3)) / np.sqrt(I) / s[:, None], "e4m3")
    hw_words, hw_scales = pack_weight(np.random.standard_normal((U, U * 3)) / np.sqrt(U), "e4m3")
    bias = bf(np.random.standard_normal(U * 3) * 0.1)
    return {"x_t": x_t,
            "h_tm1": h_tm1,
            "input_weight_words": iw_words,
            "input_weight_scales": iw_scales,
            "hidden_state_weight_words": hw_words,
            "hidden_state_weight_scales": hw_scales,
            "bias": bias}


def reference(x_t, h_tm1, input_weight_words, input_weight_scales, hidden_state_weight_words, hidden_state_weight_scales, bias):
    u = U
    x, h, b = f64(x_t), f64(h_tm1), f64(bias)
    whq = unpack_weight(hidden_state_weight_words, hidden_state_weight_scales, "e4m3")
    xg = mxq(x, 1, "e4m3") @ unpack_weight(input_weight_words, input_weight_scales, "e4m3")
    xr, xu, xh = xg[:, :u], xg[:, u:2 * u], xg[:, 2 * u:]
    hg = mxq(h, 1, "e4m3") @ whq[:, :2 * u]
    hr, hu = hg[:, :u], hg[:, u:]
    br, bu_, bh = b[:u], b[u:2 * u], b[2 * u:]
    r_t = sigmoid(xr + hr + br)
    u_t = sigmoid(xu + hu + bu_)
    cand = np.tanh(xh + (mxq(r_t * h, 1, "e4m3") @ whq[:, 2 * u:]) + bh)
    h_t = u_t * h + (1.0 - u_t) * cand
    return h_t

@@ -1,0 +1,222 @@
+from contextlib import ExitStack
+
+import concourse.mybir as mybir
+from concourse.masks import make_identity
+
+FLOPS = 2 * 128 * 2048 * (6144 + 4096 + 2048)
+
+F32 = mybir.dt.float32
+BF16 = mybir.dt.bfloat16
+U8 = mybir.dt.uint8
+U32 = mybir.dt.uint32
+I32 = mybir.dt.int32
+FP8X4 = mybir.dt.float8_e4m3fn_x4
+ADD = mybir.AluOpType.add
+MULT = mybir.AluOpType.mult
+ACT = mybir.ActivationFunctionType
+
+P = 128
+U = 2048
+NB = 512
+GROUPS = 4
+SLOTS = 12
+
+
+def tile_anothergrucell_w_kernel(tc, x_t, h_tm1, iw_words, iw_scales, hw_words, hw_scales, bias, out):
+    nc = tc.nc
+    with ExitStack() as ctx:
+        const = ctx.enter_context(tc.tile_pool(name="const", bufs=1))
+        wpool = ctx.enter_context(tc.tile_pool(name="wpool", bufs=SLOTS))
+        work = ctx.enter_context(tc.tile_pool(name="work", bufs=2))
+        psa = ctx.enter_context(tc.psum_pool(name="psa", bufs=1))
+        psb = ctx.enter_context(tc.psum_pool(name="psb", bufs=4))
+
+        plane_i = const.tile([P, 3 * U], U8, name="plane_i", align_bytes=64)
+        plane_h = const.tile([P, 3 * U], U8, name="plane_h", align_bytes=64)
+        nc.vector.memset(plane_i[:].bitcast(I32), 0)
+        nc.vector.memset(plane_h[:].bitcast(I32), 0)
+        bias_rows = const.tile([P, NB], BF16, name="bias_rows")
+        nc.vector.memset(bias_rows[:], 0.0)
+        warm_in = const.tile([P, 1], F32, name="warm_in")
+        nc.vector.memset(warm_in[:], 0.0)
+        warm_a = const.tile([P, 1], F32, name="warm_a")
+        nc.scalar.activation(out=warm_a[:], in_=warm_in[:], func=ACT.Sigmoid)
+
+        ident_f = const.tile([P, P], F32, name="ident_f")
+        make_identity(nc, ident_f[:])
+        ident_b = const.tile([P, P], BF16, name="ident_b")
+        make_identity(nc, ident_b[:])
+
+        x_sb = const.tile([P, U], BF16, name="x_sb")
+        h_sb = const.tile([P, U], BF16, name="h_sb")
+        nc.sync.dma_start(out=x_sb[:], in_=x_t)
+        nc.sync.dma_start(out=h_sb[:], in_=h_tm1)
+        nc.scalar.dma_start(out=bias_rows[0:12, :], in_=bias.rearrange("(c n) -> c n", n=NB))
+        for plane, scales in ((plane_i, iw_scales), (plane_h, hw_scales)):
+            for q in range(4):
+                nc.sync.dma_start(
+                    out=plane[32 * q:32 * q + 16, :].bitcast(I32),
+                    in_=scales[:, 4 * q:4 * q + 4, :].bitcast(I32),
+                )
+
+        def load_rows(words, g, c0):
+            def go():
+                w = wpool.tile([P, U], U32, tag="w", name="w", align_bytes=64)
+                src = words[g].rearrange("p n t -> p (n t)")[:, 4 * c0:4 * (c0 + U)]
+                nc.sync.dma_start(out=w[:].bitcast(I32), in_=src.bitcast(I32))
+                return w
+            return go
+
+        def load_block(words, c0):
+            def go():
+                w = wpool.tile([P, GROUPS, NB], U32, tag="w", name="wb", align_bytes=64)
+                for g in range(GROUPS):
+                    src = words[g].rearrange("p n t -> p (n t)")[:, 4 * c0:4 * (c0 + NB)]
+                    nc.sync.dma_start(out=w[:, g, :].bitcast(I32), in_=src.bitcast(I32))
+                return w
+            return go
+
+        loads = []
+        for c0 in (0, U):
+            for words in (iw_words, hw_words):
+                for g in range(GROUPS):
+                    loads.append(load_rows(words, g, c0))
+        for g in range(GROUPS):
+            loads.append(load_rows(iw_words, g, 2 * U))
+        for j in range(4):
+            loads.append(load_block(hw_words, 2 * U + NB * j))
+        landed = []
+
+        def issue_next():
+            if len(landed) < len(loads):
+                landed.append(loads[len(landed)]())
+
+        for i in range(SLOTS):
+            issue_next()
+
+        def quantise(src_sb, banks, label):
+            grp = work.tile([P, 4 * NB], BF16, tag="grp", name="grp_" + label, align_bytes=64)
+            for b in range(2):
+                tp = banks(b)
+                for s in range(4):
+                    g = 2 * b + s // 2
+                    u = s % 2
+                    nc.tensor.transpose(
+                        tp[:, s, :],
+                        src_sb[:].bitcast(F32)[:, 256 * g + u:256 * (g + 1):2],
+                        ident_f[:],
+                    )
+                dst = grp[:].bitcast(F32)[:, NB * b:NB * (b + 1)].rearrange("p (a r u) -> p a r u", a=2, u=2)
+                src = tp[:].rearrange("p (a u) r -> p a r u", u=2)
+                if b == 0:
+                    nc.vector.tensor_copy(out=dst, in_=src)
+                else:
+                    nc.scalar.copy(out=dst, in_=src)
+            codes = const.tile([P, NB], U32, name="codes_" + label, align_bytes=64)
+            scl = const.tile([P, NB], U8, name="scl_" + label, align_bytes=64)
+            nc.vector.quantize_mx(out=codes[:].bitcast(FP8X4), scales=scl[:], in_=grp[:])
+            return codes, scl
+
+        def bank_b(label):
+            def go(b):
+                t = psb.tile([P, 4, P], F32, tag="b", name="tp_" + label)
+                return t
+            return go
+
+        def bank_a(label):
+            def go(b):
+                t = psa.tile([P, 4, P], F32, tag="a%d" % b, name="tp_" + label)
+                return t
+            return go
+
+        xq = quantise(x_sb, bank_b("x"), "x")
+        hq = quantise(h_sb, bank_b("h"), "h")
+
+        bias_sb = const.tile([P, 3 * U], BF16, name="bias_sb")
+        for c in range(12):
+            bp = psb.tile([P, NB], F32, tag="b", name="bp")
+            nc.tensor.matmul(
+                out=bp[:],
+                lhsT=ident_b[:, c:c + 1].to_broadcast([P, P]),
+                rhs=bias_rows[:],
+                start=True,
+                stop=True,
+            )
+            nc.scalar.copy(out=bias_sb[:, NB * c:NB * (c + 1)], in_=bp[:])
+
+        def mx_pass(acc, act, g, w_ap, plane, c0, start, stop):
+            codes, scl = act
+            nc.tensor.matmul_mx(
+                out=acc[:],
+                lhsT=codes[:, P * g:P * (g + 1)].bitcast(FP8X4),
+                lhsT_scale=scl[:, P * g:P * (g + 1)],
+                rhs=w_ap.bitcast(FP8X4),
+                rhs_scale=plane[4 * g:P, c0:c0 + NB],
+                start=start,
+                stop=stop,
+            )
+
+        used = [0]
+
+        def gate_passes(accs, c0, sides):
+            n = len(sides) * GROUPS
+            k = 0
+            for act, plane in sides:
+                for g in range(GROUPS):
+                    w = landed[used[0]]
+                    used[0] += 1
+                    for j in range(4):
+                        mx_pass(accs[j], act, g, w[:, NB * j:NB * (j + 1)], plane, c0 + NB * j, k == 0, k == n - 1)
+                    k += 1
+                    issue_next()
+
+        acc_r = [psa.tile([P, NB], F32, tag="a%d" % j, name="acc_r%d" % j) for j in range(4)]
+        gate_passes(acc_r, 0, ((xq, plane_i), (hq, plane_h)))
+        rh_sb = const.tile([P, U], BF16, name="rh_sb")
+        for j in range(4):
+            cols = slice(NB * j, NB * (j + 1))
+            z = work.tile([P, NB], F32, tag="z", name="z")
+            nc.vector.tensor_tensor(out=z[:], in0=acc_r[j][:], in1=bias_sb[:, cols], op=ADD)
+            r = work.tile([P, NB], F32, tag="r", name="r")
+            nc.scalar.activation(out=r[:], in_=z[:], func=ACT.Sigmoid)
+            nc.vector.tensor_tensor(out=rh_sb[:, cols], in0=r[:], in1=h_sb[:, cols], op=MULT)
+        rq = quantise(rh_sb, bank_a("rh"), "rh")
+
+        acc_u = [psb.tile([P, NB], F32, tag="b", name="acc_u%d" % j) for j in range(4)]
+        gate_passes(acc_u, U, ((xq, plane_i), (hq, plane_h)))
+        uh_sb = const.tile([P, U], F32, name="uh_sb")
+        nu_sb = const.tile([P, U], F32, name="nu_sb")
+        for j in range(4):
+            cols = slice(NB * j, NB * (j + 1))
+            z = work.tile([P, NB], F32, tag="z", name="z")
+            nc.vector.tensor_tensor(out=z[:], in0=acc_u[j][:], in1=bias_sb[:, U + NB * j:U + NB * (j + 1)], op=ADD)
+            ug = work.tile([P, NB], F32, tag="r", name="ug")
+            nc.scalar.activation(out=ug[:], in_=z[:], func=ACT.Sigmoid)
+            nc.scalar.activation(out=nu_sb[:, cols], in_=z[:], func=ACT.Sigmoid, scale=-1.0)
+            nc.vector.tensor_tensor(out=uh_sb[:, cols], in0=ug[:], in1=h_sb[:, cols], op=MULT)
+        warm_b = const.tile([P, 1], F32, name="warm_b")
+        nc.scalar.activation(out=warm_b[:], in_=nu_sb[:, U - 1:U], func=ACT.Tanh)
+
+        acc_x = [psa.tile([P, NB], F32, tag="a%d" % j, name="acc_x%d" % j) for j in range(4)]
+        gate_passes(acc_x, 2 * U, ((xq, plane_i),))
+        xhb = const.tile([P, U], F32, name="xhb")
+        for j in range(4):
+            cols = slice(NB * j, NB * (j + 1))
+            nc.vector.tensor_tensor(out=xhb[:, cols], in0=acc_x[j][:], in1=bias_sb[:, 2 * U + NB * j:2 * U + NB * (j + 1)], op=ADD)
+
+        for j in range(4):
+            cols = slice(NB * j, NB * (j + 1))
+            w = landed[used[0]]
+            used[0] += 1
+            pc = psb.tile([P, NB], F32, tag="b", name="pc")
+            for g in range(GROUPS):
+                mx_pass(pc, rq, g, w[:, g, :], plane_h, 2 * U + NB * j, g == 0, g == GROUPS - 1)
+            z = work.tile([P, NB], F32, tag="z", name="z")
+            nc.vector.tensor_tensor(out=z[:], in0=pc[:], in1=xhb[:, cols], op=ADD)
+            cand = work.tile([P, NB], F32, tag="cand", name="cand")
+            nc.scalar.activation(out=cand[:], in_=z[:], func=ACT.Tanh)
+            m = work.tile([P, NB], F32, tag="m", name="m")
+            nc.vector.tensor_tensor(out=m[:], in0=cand[:], in1=nu_sb[:, cols], op=MULT)
+            o = work.tile([P, NB], F32, tag="o", name="o")
+            nc.vector.tensor_tensor(out=o[:], in0=m[:], in1=uh_sb[:, cols], op=ADD)
+            nc.sync.dma_start(out=out[:, cols], in_=o[:])

@@ -44,8 +44,6 @@ def tile_anothergrucell_w_kernel(tc, x_t, h_tm1, iw_words, iw_scales, hw_words, 
 
         ident_f = const.tile([P, P], F32, name="ident_f")
         make_identity(nc, ident_f[:])
-        ident_b = const.tile([P, P], BF16, name="ident_b")
-        make_identity(nc, ident_b[:])
 
         x_sb = const.tile([P, U], BF16, name="x_sb")
         h_sb = const.tile([P, U], BF16, name="h_sb")
@@ -54,10 +52,13 @@ def tile_anothergrucell_w_kernel(tc, x_t, h_tm1, iw_words, iw_scales, hw_words, 
         nc.scalar.dma_start(out=bias_rows[0:12, :], in_=bias.rearrange("(c n) -> c n", n=NB))
         for plane, scales in ((plane_i, iw_scales), (plane_h, hw_scales)):
             for q in range(4):
-                nc.sync.dma_start(
-                    out=plane[32 * q:32 * q + 16, :].bitcast(I32),
-                    in_=scales[:, 4 * q:4 * q + 4, :].bitcast(I32),
+                nc.gpsimd.dma_start(
+                    out=plane[32 * q:32 * q + 16, :].bitcast(F32),
+                    in_=scales[:, 4 * q:4 * q + 4, :].bitcast(F32),
                 )
+
+        ident_b = const.tile([P, P], BF16, name="ident_b")
+        make_identity(nc, ident_b[:])
 
         def load_rows(words, g, c0):
             def go():

@@ -19,7 +19,7 @@ P = 128
 U = 2048
 NB = 512
 GROUPS = 4
-SLOTS = 12
+SLOTS = 14
 
 
 def tile_anothergrucell_w_kernel(tc, x_t, h_tm1, iw_words, iw_scales, hw_words, hw_scales, bias, out):
@@ -44,21 +44,22 @@ def tile_anothergrucell_w_kernel(tc, x_t, h_tm1, iw_words, iw_scales, hw_words, 
 
         ident_f = const.tile([P, P], F32, name="ident_f")
         make_identity(nc, ident_f[:])
+        ident_b = const.tile([P, P], BF16, name="ident_b")
+        make_identity(nc, ident_b[:])
 
         x_sb = const.tile([P, U], BF16, name="x_sb")
         h_sb = const.tile([P, U], BF16, name="h_sb")
-        nc.sync.dma_start(out=x_sb[:], in_=x_t)
-        nc.sync.dma_start(out=h_sb[:], in_=h_tm1)
         nc.scalar.dma_start(out=bias_rows[0:12, :], in_=bias.rearrange("(c n) -> c n", n=NB))
-        for plane, scales in ((plane_i, iw_scales), (plane_h, hw_scales)):
+
+        def load_scales(plane, scales):
             for q in range(4):
-                nc.gpsimd.dma_start(
-                    out=plane[32 * q:32 * q + 16, :].bitcast(F32),
-                    in_=scales[:, 4 * q:4 * q + 4, :].bitcast(F32),
+                nc.sync.dma_start(
+                    out=plane[32 * q:32 * q + 16, :].bitcast(I32),
+                    in_=scales[:, 4 * q:4 * q + 4, :].bitcast(I32),
                 )
 
-        ident_b = const.tile([P, P], BF16, name="ident_b")
-        make_identity(nc, ident_b[:])
+        nc.sync.dma_start(out=x_sb[:], in_=x_t)
+        load_scales(plane_i, iw_scales)
 
         def load_rows(words, g, c0):
             def go():
@@ -93,6 +94,9 @@ def tile_anothergrucell_w_kernel(tc, x_t, h_tm1, iw_words, iw_scales, hw_words, 
                 landed.append(loads[len(landed)]())
 
         for i in range(SLOTS):
+            if i == GROUPS:
+                nc.sync.dma_start(out=h_sb[:], in_=h_tm1)
+                load_scales(plane_h, hw_scales)
             issue_next()
 
         def quantise(src_sb, banks, label):
@@ -198,26 +202,35 @@ def tile_anothergrucell_w_kernel(tc, x_t, h_tm1, iw_words, iw_scales, hw_words, 
         warm_b = const.tile([P, 1], F32, name="warm_b")
         nc.scalar.activation(out=warm_b[:], in_=nu_sb[:, U - 1:U], func=ACT.Tanh)
 
-        acc_x = [psa.tile([P, NB], F32, tag="a%d" % j, name="acc_x%d" % j) for j in range(4)]
-        gate_passes(acc_x, 2 * U, ((xq, plane_i),))
-        xhb = const.tile([P, U], F32, name="xhb")
-        for j in range(4):
-            cols = slice(NB * j, NB * (j + 1))
-            nc.vector.tensor_tensor(out=xhb[:, cols], in0=acc_x[j][:], in1=bias_sb[:, 2 * U + NB * j:2 * U + NB * (j + 1)], op=ADD)
-
-        for j in range(4):
-            cols = slice(NB * j, NB * (j + 1))
+        acc_c = [psa.tile([P, NB], F32, tag="a%d" % j, name="acc_c%d" % j) for j in range(4)]
+        for g in range(GROUPS):
             w = landed[used[0]]
             used[0] += 1
-            pc = psb.tile([P, NB], F32, tag="b", name="pc")
+            for j in range(4):
+                mx_pass(acc_c[j], xq, g, w[:, NB * j:NB * (j + 1)], plane_i, 2 * U + NB * j, g == 0, False)
+            issue_next()
+
+        HALF = NB // 2
+        for j in range(4):
+            w = landed[used[0]]
+            used[0] += 1
             for g in range(GROUPS):
-                mx_pass(pc, rq, g, w[:, g, :], plane_h, 2 * U + NB * j, g == 0, g == GROUPS - 1)
+                mx_pass(acc_c[j], rq, g, w[:, g, :], plane_h, 2 * U + NB * j, False, g == GROUPS - 1)
             z = work.tile([P, NB], F32, tag="z", name="z")
-            nc.vector.tensor_tensor(out=z[:], in0=pc[:], in1=xhb[:, cols], op=ADD)
             cand = work.tile([P, NB], F32, tag="cand", name="cand")
-            nc.scalar.activation(out=cand[:], in_=z[:], func=ACT.Tanh)
             m = work.tile([P, NB], F32, tag="m", name="m")
-            nc.vector.tensor_tensor(out=m[:], in0=cand[:], in1=nu_sb[:, cols], op=MULT)
             o = work.tile([P, NB], F32, tag="o", name="o")
-            nc.vector.tensor_tensor(out=o[:], in0=m[:], in1=uh_sb[:, cols], op=ADD)
-            nc.sync.dma_start(out=out[:, cols], in_=o[:])
+            for s in range(2):
+                loc = slice(HALF * s, HALF * (s + 1))
+                c0 = NB * j + HALF * s
+                nc.vector.tensor_tensor(out=z[:, loc], in0=acc_c[j][:, loc], in1=bias_sb[:, 2 * U + c0:2 * U + c0 + HALF], op=ADD)
+                nc.scalar.activation(out=cand[:, loc], in_=z[:, loc], func=ACT.Tanh)
+            for s in range(2):
+                loc = slice(HALF * s, HALF * (s + 1))
+                c0 = NB * j + HALF * s
+                nc.vector.tensor_tensor(out=m[:, loc], in0=cand[:, loc], in1=nu_sb[:, c0:c0 + HALF], op=MULT)
+                nc.vector.tensor_tensor(out=o[:, loc], in0=m[:, loc], in1=uh_sb[:, c0:c0 + HALF], op=ADD)
+                if j == 3:
+                    nc.sync.dma_start(out=out[:, c0:c0 + HALF], in_=o[:, loc])
+            if j < 3:
+                nc.sync.dma_start(out=out[:, NB * j:NB * (j + 1)], in_=o[:])

@@ -49,17 +49,17 @@ def tile_anothergrucell_w_kernel(tc, x_t, h_tm1, iw_words, iw_scales, hw_words, 
 
         x_sb = const.tile([P, U], BF16, name="x_sb")
         h_sb = const.tile([P, U], BF16, name="h_sb")
-        nc.scalar.dma_start(out=bias_rows[0:12, :], in_=bias.rearrange("(c n) -> c n", n=NB))
-
-        def load_scales(plane, scales):
-            for q in range(4):
-                nc.sync.dma_start(
-                    out=plane[32 * q:32 * q + 16, :].bitcast(I32),
-                    in_=scales[:, 4 * q:4 * q + 4, :].bitcast(I32),
-                )
-
         nc.sync.dma_start(out=x_sb[:], in_=x_t)
-        load_scales(plane_i, iw_scales)
+        nc.sync.dma_start(out=h_sb[:], in_=h_tm1)
+        nc.scalar.dma_start(out=bias_rows[0:12, :], in_=bias.rearrange("(c n) -> c n", n=NB))
+        SC = 3 * U // 2
+        for part in range(2):
+            for plane, scales in ((plane_i, iw_scales), (plane_h, hw_scales)):
+                for q in range(4):
+                    nc.sync.dma_start(
+                        out=plane[32 * q:32 * q + 16, SC * part:SC * (part + 1)].bitcast(I32),
+                        in_=scales[:, 4 * q:4 * q + 4, SC * part:SC * (part + 1)].bitcast(I32),
+                    )
 
         def load_rows(words, g, c0):
             def go():
@@ -94,9 +94,6 @@ def tile_anothergrucell_w_kernel(tc, x_t, h_tm1, iw_words, iw_scales, hw_words, 
                 landed.append(loads[len(landed)]())
 
         for i in range(SLOTS):
-            if i == GROUPS:
-                nc.sync.dma_start(out=h_sb[:], in_=h_tm1)
-                load_scales(plane_h, hw_scales)
             issue_next()
 
         def quantise(src_sb, banks, label):

@@ -52,14 +52,12 @@ def tile_anothergrucell_w_kernel(tc, x_t, h_tm1, iw_words, iw_scales, hw_words, 
         nc.sync.dma_start(out=x_sb[:], in_=x_t)
         nc.sync.dma_start(out=h_sb[:], in_=h_tm1)
         nc.scalar.dma_start(out=bias_rows[0:12, :], in_=bias.rearrange("(c n) -> c n", n=NB))
-        SC = 3 * U // 2
-        for part in range(2):
-            for plane, scales in ((plane_i, iw_scales), (plane_h, hw_scales)):
-                for q in range(4):
-                    nc.sync.dma_start(
-                        out=plane[32 * q:32 * q + 16, SC * part:SC * (part + 1)].bitcast(I32),
-                        in_=scales[:, 4 * q:4 * q + 4, SC * part:SC * (part + 1)].bitcast(I32),
-                    )
+        for plane, scales in ((plane_i, iw_scales), (plane_h, hw_scales)):
+            for q in range(4):
+                nc.sync.dma_start(
+                    out=plane[32 * q:32 * q + 16, :].bitcast(I32),
+                    in_=scales[:, 4 * q:4 * q + 4, :].bitcast(I32),
+                )
 
         def load_rows(words, g, c0):
             def go():

@@ -52,12 +52,17 @@ def tile_anothergrucell_w_kernel(tc, x_t, h_tm1, iw_words, iw_scales, hw_words, 
         nc.sync.dma_start(out=x_sb[:], in_=x_t)
         nc.sync.dma_start(out=h_sb[:], in_=h_tm1)
         nc.scalar.dma_start(out=bias_rows[0:12, :], in_=bias.rearrange("(c n) -> c n", n=NB))
-        for plane, scales in ((plane_i, iw_scales), (plane_h, hw_scales)):
-            for q in range(4):
-                nc.sync.dma_start(
-                    out=plane[32 * q:32 * q + 16, :].bitcast(I32),
-                    in_=scales[:, 4 * q:4 * q + 4, :].bitcast(I32),
-                )
+        for i in range(4):
+            q = i
+            nc.sync.dma_start(
+                out=plane_i[32 * q:32 * q + 16, :].bitcast(I32),
+                in_=iw_scales[:, 4 * q:4 * q + 4, :].bitcast(I32),
+            )
+            q = (i + 2) % 4
+            nc.scalar.dma_start(
+                out=plane_h[32 * q:32 * q + 16, :].bitcast(F32),
+                in_=hw_scales[:, 4 * q:4 * q + 4, :].bitcast(F32),
+            )
 
         def load_rows(words, g, c0):
             def go():

@@ -52,17 +52,12 @@ def tile_anothergrucell_w_kernel(tc, x_t, h_tm1, iw_words, iw_scales, hw_words, 
         nc.sync.dma_start(out=x_sb[:], in_=x_t)
         nc.sync.dma_start(out=h_sb[:], in_=h_tm1)
         nc.scalar.dma_start(out=bias_rows[0:12, :], in_=bias.rearrange("(c n) -> c n", n=NB))
-        for i in range(4):
-            q = i
-            nc.sync.dma_start(
-                out=plane_i[32 * q:32 * q + 16, :].bitcast(I32),
-                in_=iw_scales[:, 4 * q:4 * q + 4, :].bitcast(I32),
-            )
-            q = (i + 2) % 4
-            nc.scalar.dma_start(
-                out=plane_h[32 * q:32 * q + 16, :].bitcast(F32),
-                in_=hw_scales[:, 4 * q:4 * q + 4, :].bitcast(F32),
-            )
+        for plane, scales in ((plane_i, iw_scales), (plane_h, hw_scales)):
+            for q in (0, 2, 1, 3):
+                nc.sync.dma_start(
+                    out=plane[32 * q:32 * q + 16, :].bitcast(I32),
+                    in_=scales[:, 4 * q:4 * q + 4, :].bitcast(I32),
+                )
 
         def load_rows(words, g, c0):
             def go():

@@ -50,14 +50,15 @@ def tile_anothergrucell_w_kernel(tc, x_t, h_tm1, iw_words, iw_scales, hw_words, 
         x_sb = const.tile([P, U], BF16, name="x_sb")
         h_sb = const.tile([P, U], BF16, name="h_sb")
         nc.sync.dma_start(out=x_sb[:], in_=x_t)
-        nc.sync.dma_start(out=h_sb[:], in_=h_tm1)
         nc.scalar.dma_start(out=bias_rows[0:12, :], in_=bias.rearrange("(c n) -> c n", n=NB))
-        for plane, scales in ((plane_i, iw_scales), (plane_h, hw_scales)):
-            for q in (0, 2, 1, 3):
-                nc.sync.dma_start(
-                    out=plane[32 * q:32 * q + 16, :].bitcast(I32),
-                    in_=scales[:, 4 * q:4 * q + 4, :].bitcast(I32),
-                )
+        for quads in ((2, 3), (0, 1)):
+            for plane, scales in ((plane_i, iw_scales), (plane_h, hw_scales)):
+                for q in quads:
+                    nc.sync.dma_start(
+                        out=plane[32 * q:32 * q + 16, :].bitcast(I32),
+                        in_=scales[:, 4 * q:4 * q + 4, :].bitcast(I32),
+                    )
+        nc.sync.dma_start(out=h_sb[:], in_=h_tm1)
 
         def load_rows(words, g, c0):
             def go():

@@ -19,14 +19,13 @@ P = 128
 U = 2048
 NB = 512
 GROUPS = 4
-SLOTS = 14
 
 
 def tile_anothergrucell_w_kernel(tc, x_t, h_tm1, iw_words, iw_scales, hw_words, hw_scales, bias, out):
     nc = tc.nc
     with ExitStack() as ctx:
         const = ctx.enter_context(tc.tile_pool(name="const", bufs=1))
-        wpool = ctx.enter_context(tc.tile_pool(name="wpool", bufs=SLOTS))
+        wpool = ctx.enter_context(tc.tile_pool(name="wpool", bufs=4))
         work = ctx.enter_context(tc.tile_pool(name="work", bufs=2))
         psa = ctx.enter_context(tc.psum_pool(name="psa", bufs=1))
         psb = ctx.enter_context(tc.psum_pool(name="psb", bufs=4))
@@ -47,7 +46,7 @@ def tile_anothergrucell_w_kernel(tc, x_t, h_tm1, iw_words, iw_scales, hw_words, 
         ident_b = const.tile([P, P], BF16, name="ident_b")
         make_identity(nc, ident_b[:])
 
-        x_sb = const.tile([P, U], BF16, name="x_sb")
+        x_sb = const.tile([P, U], BF16, tag="xr", name="x_sb")
         h_sb = const.tile([P, U], BF16, name="h_sb")
         nc.sync.dma_start(out=x_sb[:], in_=x_t)
         nc.scalar.dma_start(out=bias_rows[0:12, :], in_=bias.rearrange("(c n) -> c n", n=NB))
@@ -60,40 +59,25 @@ def tile_anothergrucell_w_kernel(tc, x_t, h_tm1, iw_words, iw_scales, hw_words, 
                     )
         nc.sync.dma_start(out=h_sb[:], in_=h_tm1)
 
-        def load_rows(words, g, c0):
-            def go():
-                w = wpool.tile([P, U], U32, tag="w", name="w", align_bytes=64)
-                src = words[g].rearrange("p n t -> p (n t)")[:, 4 * c0:4 * (c0 + U)]
-                nc.sync.dma_start(out=w[:].bitcast(I32), in_=src.bitcast(I32))
-                return w
-            return go
+        def load(tile, words, g, c0, width):
+            src = words[g].rearrange("p n t -> p (n t)")[:, 4 * c0:4 * (c0 + width)]
+            nc.sync.dma_start(out=tile.bitcast(I32), in_=src.bitcast(I32))
 
-        def load_block(words, c0):
-            def go():
-                w = wpool.tile([P, GROUPS, NB], U32, tag="w", name="wb", align_bytes=64)
-                for g in range(GROUPS):
-                    src = words[g].rearrange("p n t -> p (n t)")[:, 4 * c0:4 * (c0 + NB)]
-                    nc.sync.dma_start(out=w[:, g, :].bitcast(I32), in_=src.bitcast(I32))
-                return w
-            return go
-
-        loads = []
-        for c0 in (0, U):
-            for words in (iw_words, hw_words):
-                for g in range(GROUPS):
-                    loads.append(load_rows(words, g, c0))
+        w_iru = []
+        w_hr = []
+        w_huc = []
         for g in range(GROUPS):
-            loads.append(load_rows(iw_words, g, 2 * U))
-        for j in range(4):
-            loads.append(load_block(hw_words, 2 * U + NB * j))
-        landed = []
-
-        def issue_next():
-            if len(landed) < len(loads):
-                landed.append(loads[len(landed)]())
-
-        for i in range(SLOTS):
-            issue_next()
+            w = wpool.tile([P, 2 * U], U32, tag="wide", name="w_iru", align_bytes=64)
+            load(w[:], iw_words, g, 0, 2 * U)
+            w_iru.append(w)
+        for g in range(GROUPS):
+            w = wpool.tile([P, U], U32, tag="reset", name="w_hr", align_bytes=64)
+            load(w[:], hw_words, g, 0, U)
+            w_hr.append(w)
+        for g in range(GROUPS):
+            w = wpool.tile([P, U + 2 * NB], U32, tag="update", name="w_huc", align_bytes=64)
+            load(w[:], hw_words, g, U, U + 2 * NB)
+            w_huc.append(w)
 
         def quantise(src_sb, banks, label):
             grp = work.tile([P, 4 * NB], BF16, tag="grp", name="grp_" + label, align_bytes=64)
@@ -157,23 +141,27 @@ def tile_anothergrucell_w_kernel(tc, x_t, h_tm1, iw_words, iw_scales, hw_words, 
                 stop=stop,
             )
 
-        used = [0]
-
-        def gate_passes(accs, c0, sides):
-            n = len(sides) * GROUPS
-            k = 0
-            for act, plane in sides:
-                for g in range(GROUPS):
-                    w = landed[used[0]]
-                    used[0] += 1
-                    for j in range(4):
-                        mx_pass(accs[j], act, g, w[:, NB * j:NB * (j + 1)], plane, c0 + NB * j, k == 0, k == n - 1)
-                    k += 1
-                    issue_next()
-
         acc_r = [psa.tile([P, NB], F32, tag="a%d" % j, name="acc_r%d" % j) for j in range(4)]
-        gate_passes(acc_r, 0, ((xq, plane_i), (hq, plane_h)))
-        rh_sb = const.tile([P, U], BF16, name="rh_sb")
+        acc_u = [psb.tile([P, NB], F32, tag="b", name="acc_u%d" % j) for j in range(4)]
+        for g in range(GROUPS):
+            for j, acc in enumerate(acc_r + acc_u):
+                mx_pass(acc, xq, g, w_iru[g][:, NB * j:NB * (j + 1)], plane_i, NB * j, g == 0, False)
+
+        w_ic = []
+        for c0 in (2 * U, 2 * U + 2 * NB):
+            w = wpool.tile([P, GROUPS, 2 * NB], U32, tag="wide", name="w_ic", align_bytes=64)
+            for g in range(GROUPS):
+                load(w[:, g, :], iw_words, g, c0, 2 * NB)
+            w_ic.append(w)
+        w_hc = wpool.tile([P, 2, GROUPS, NB], U32, tag="wide", name="w_hc", align_bytes=64)
+        for b in range(2):
+            for g in range(GROUPS):
+                load(w_hc[:, b, g, :], hw_words, g, 2 * U + NB * (2 + b), NB)
+
+        for g in range(GROUPS):
+            for j in range(4):
+                mx_pass(acc_r[j], hq, g, w_hr[g][:, NB * j:NB * (j + 1)], plane_h, NB * j, False, g == GROUPS - 1)
+        rh_sb = const.tile([P, U], BF16, tag="xr", name="rh_sb")
         for j in range(4):
             cols = slice(NB * j, NB * (j + 1))
             z = work.tile([P, NB], F32, tag="z", name="z")
@@ -183,8 +171,9 @@ def tile_anothergrucell_w_kernel(tc, x_t, h_tm1, iw_words, iw_scales, hw_words, 
             nc.vector.tensor_tensor(out=rh_sb[:, cols], in0=r[:], in1=h_sb[:, cols], op=MULT)
         rq = quantise(rh_sb, bank_a("rh"), "rh")
 
-        acc_u = [psb.tile([P, NB], F32, tag="b", name="acc_u%d" % j) for j in range(4)]
-        gate_passes(acc_u, U, ((xq, plane_i), (hq, plane_h)))
+        for g in range(GROUPS):
+            for j in range(4):
+                mx_pass(acc_u[j], hq, g, w_huc[g][:, NB * j:NB * (j + 1)], plane_h, U + NB * j, False, g == GROUPS - 1)
         uh_sb = const.tile([P, U], F32, name="uh_sb")
         nu_sb = const.tile([P, U], F32, name="nu_sb")
         for j in range(4):
@@ -198,35 +187,64 @@ def tile_anothergrucell_w_kernel(tc, x_t, h_tm1, iw_words, iw_scales, hw_words, 
         warm_b = const.tile([P, 1], F32, name="warm_b")
         nc.scalar.activation(out=warm_b[:], in_=nu_sb[:, U - 1:U], func=ACT.Tanh)
 
-        acc_c = [psa.tile([P, NB], F32, tag="a%d" % j, name="acc_c%d" % j) for j in range(4)]
-        for g in range(GROUPS):
-            w = landed[used[0]]
-            used[0] += 1
-            for j in range(4):
-                mx_pass(acc_c[j], xq, g, w[:, NB * j:NB * (j + 1)], plane_i, 2 * U + NB * j, g == 0, False)
-            issue_next()
-
         HALF = NB // 2
-        for j in range(4):
-            w = landed[used[0]]
-            used[0] += 1
+        acc_c = [psa.tile([P, NB], F32, tag="a%d" % j, name="acc_c%d" % j) for j in range(4)]
+        out_sb = const.tile([P, U], F32, name="out_sb")
+        cand_sb = {}
+
+        def input_passes(b):
             for g in range(GROUPS):
-                mx_pass(acc_c[j], rq, g, w[:, g, :], plane_h, 2 * U + NB * j, False, g == GROUPS - 1)
+                for j in (2 * b, 2 * b + 1):
+                    mx_pass(acc_c[j], xq, g, w_ic[b][:, g, NB * (j - 2 * b):NB * (j - 2 * b + 1)], plane_i, 2 * U + NB * j, g == 0, False)
+
+        def hidden_passes(j):
+            for g in range(GROUPS):
+                w_ap = w_huc[g][:, U + NB * j:U + NB * (j + 1)] if j < 2 else w_hc[:, j - 2, g, :]
+                mx_pass(acc_c[j], rq, g, w_ap, plane_h, 2 * U + NB * j, False, g == GROUPS - 1)
+
+        def add_bias(j):
             z = work.tile([P, NB], F32, tag="z", name="z")
-            cand = work.tile([P, NB], F32, tag="cand", name="cand")
-            m = work.tile([P, NB], F32, tag="m", name="m")
-            o = work.tile([P, NB], F32, tag="o", name="o")
-            for s in range(2):
-                loc = slice(HALF * s, HALF * (s + 1))
-                c0 = NB * j + HALF * s
-                nc.vector.tensor_tensor(out=z[:, loc], in0=acc_c[j][:, loc], in1=bias_sb[:, 2 * U + c0:2 * U + c0 + HALF], op=ADD)
-                nc.scalar.activation(out=cand[:, loc], in_=z[:, loc], func=ACT.Tanh)
-            for s in range(2):
-                loc = slice(HALF * s, HALF * (s + 1))
-                c0 = NB * j + HALF * s
-                nc.vector.tensor_tensor(out=m[:, loc], in0=cand[:, loc], in1=nu_sb[:, c0:c0 + HALF], op=MULT)
-                nc.vector.tensor_tensor(out=o[:, loc], in0=m[:, loc], in1=uh_sb[:, c0:c0 + HALF], op=ADD)
-                if j == 3:
-                    nc.sync.dma_start(out=out[:, c0:c0 + HALF], in_=o[:, loc])
-            if j < 3:
-                nc.sync.dma_start(out=out[:, NB * j:NB * (j + 1)], in_=o[:])
+            cand_sb[j] = work.tile([P, NB], F32, tag="cand", name="cand")
+            for h in range(2):
+                loc = slice(HALF * h, HALF * (h + 1))
+                c0 = 2 * U + NB * j + HALF * h
+                nc.vector.tensor_tensor(out=z[:, loc], in0=acc_c[j][:, loc], in1=bias_sb[:, c0:c0 + HALF], op=ADD)
+                nc.scalar.activation(out=cand_sb[j][:, loc], in_=z[:, loc], func=ACT.Tanh)
+
+        def multiply(j, h):
+            cols = slice(NB * j + HALF * h, NB * j + HALF * (h + 1))
+            nc.vector.tensor_tensor(out=out_sb[:, cols], in0=cand_sb[j][:, HALF * h:HALF * (h + 1)], in1=nu_sb[:, cols], op=MULT)
+
+        def finish(j, h):
+            cols = slice(NB * j + HALF * h, NB * j + HALF * (h + 1))
+            nc.vector.tensor_tensor(out=out_sb[:, cols], in0=out_sb[:, cols], in1=uh_sb[:, cols], op=ADD)
+
+        def store(c0, c1):
+            nc.sync.dma_start(out=out[:, c0:c1], in_=out_sb[:, c0:c1])
+
+        with tc.manual_schedule(engines={mybir.EngineType.DVE}):
+            input_passes(0)
+            hidden_passes(0)
+            hidden_passes(1)
+            for j in (0, 1):
+                add_bias(j)
+            for step in (multiply, finish):
+                for j in (0, 1):
+                    step(j, 0)
+                    step(j, 1)
+            store(0, 2 * NB)
+            input_passes(1)
+            hidden_passes(2)
+            add_bias(2)
+            multiply(2, 0)
+            multiply(2, 1)
+            finish(2, 0)
+            hidden_passes(3)
+            add_bias(3)
+            finish(2, 1)
+            store(2 * NB, 3 * NB)
+            multiply(3, 0)
+            multiply(3, 1)
+            for h in range(2):
+                finish(3, h)
+                store(3 * NB + HALF * h, 3 * NB + HALF * (h + 1))

@@ -132,11 +132,11 @@ def tile_anothergrucell_w_kernel(tc, x_t, h_tm1, iw_words, iw_scales, hw_words, 
         def mx_pass(acc, act, g, w_ap, plane, c0, start, stop):
             codes, scl = act
             nc.tensor.matmul_mx(
-                out=acc[:],
+                out=acc,
                 lhsT=codes[:, P * g:P * (g + 1)].bitcast(FP8X4),
                 lhsT_scale=scl[:, P * g:P * (g + 1)],
                 rhs=w_ap.bitcast(FP8X4),
-                rhs_scale=plane[4 * g:P, c0:c0 + NB],
+                rhs_scale=plane[4 * g:P, c0:c0 + w_ap.shape[1]],
                 start=start,
                 stop=stop,
             )
@@ -145,7 +145,7 @@ def tile_anothergrucell_w_kernel(tc, x_t, h_tm1, iw_words, iw_scales, hw_words, 
         acc_u = [psb.tile([P, NB], F32, tag="b", name="acc_u%d" % j) for j in range(4)]
         for g in range(GROUPS):
             for j, acc in enumerate(acc_r + acc_u):
-                mx_pass(acc, xq, g, w_iru[g][:, NB * j:NB * (j + 1)], plane_i, NB * j, g == 0, False)
+                mx_pass(acc[:], xq, g, w_iru[g][:, NB * j:NB * (j + 1)], plane_i, NB * j, g == 0, False)
 
         w_ic = []
         for c0 in (2 * U, 2 * U + 2 * NB):
@@ -154,13 +154,14 @@ def tile_anothergrucell_w_kernel(tc, x_t, h_tm1, iw_words, iw_scales, hw_words, 
                 load(w[:, g, :], iw_words, g, c0, 2 * NB)
             w_ic.append(w)
         w_hc = wpool.tile([P, 2, GROUPS, NB], U32, tag="wide", name="w_hc", align_bytes=64)
-        for b in range(2):
-            for g in range(GROUPS):
-                load(w_hc[:, b, g, :], hw_words, g, 2 * U + NB * (2 + b), NB)
+        pieces = [(0, g, 0, NB) for g in range(GROUPS)] + [(1, 0, 0, NB)]
+        pieces += [(1, g, a, NB // 2) for a in (0, NB // 2) for g in range(1, GROUPS)]
+        for b, g, a, width in pieces:
+            load(w_hc[:, b, g, a:a + width], hw_words, g, 2 * U + NB * (2 + b) + a, width)
 
         for g in range(GROUPS):
             for j in range(4):
-                mx_pass(acc_r[j], hq, g, w_hr[g][:, NB * j:NB * (j + 1)], plane_h, NB * j, False, g == GROUPS - 1)
+                mx_pass(acc_r[j][:], hq, g, w_hr[g][:, NB * j:NB * (j + 1)], plane_h, NB * j, False, g == GROUPS - 1)
         rh_sb = const.tile([P, U], BF16, tag="xr", name="rh_sb")
         for j in range(4):
             cols = slice(NB * j, NB * (j + 1))
@@ -173,7 +174,7 @@ def tile_anothergrucell_w_kernel(tc, x_t, h_tm1, iw_words, iw_scales, hw_words, 
 
         for g in range(GROUPS):
             for j in range(4):
-                mx_pass(acc_u[j], hq, g, w_huc[g][:, NB * j:NB * (j + 1)], plane_h, U + NB * j, False, g == GROUPS - 1)
+                mx_pass(acc_u[j][:], hq, g, w_huc[g][:, NB * j:NB * (j + 1)], plane_h, U + NB * j, False, g == GROUPS - 1)
         uh_sb = const.tile([P, U], F32, name="uh_sb")
         nu_sb = const.tile([P, U], F32, name="nu_sb")
         for j in range(4):
@@ -188,63 +189,78 @@ def tile_anothergrucell_w_kernel(tc, x_t, h_tm1, iw_words, iw_scales, hw_words, 
         nc.scalar.activation(out=warm_b[:], in_=nu_sb[:, U - 1:U], func=ACT.Tanh)
 
         HALF = NB // 2
+        spans = [(0, NB), (NB, NB), (2 * NB, NB), (3 * NB, HALF), (3 * NB + HALF, HALF)]
         acc_c = [psa.tile([P, NB], F32, tag="a%d" % j, name="acc_c%d" % j) for j in range(4)]
+        acc_c.append(psb.tile([P, NB], F32, tag="b", name="acc_c4"))
         out_sb = const.tile([P, U], F32, name="out_sb")
-        cand_sb = {}
+        cand_sb = const.tile([P, U], F32, name="cand_sb")
 
         def input_passes(b):
             for g in range(GROUPS):
-                for j in (2 * b, 2 * b + 1):
-                    mx_pass(acc_c[j], xq, g, w_ic[b][:, g, NB * (j - 2 * b):NB * (j - 2 * b + 1)], plane_i, 2 * U + NB * j, g == 0, False)
+                for acc, (c0, width) in zip(acc_c, spans):
+                    lo = c0 - 2 * NB * b
+                    if 0 <= lo < 2 * NB:
+                        mx_pass(acc[:, :width], xq, g, w_ic[b][:, g, lo:lo + width], plane_i, 2 * U + c0, g == 0, False)
 
-        def hidden_passes(j):
-            for g in range(GROUPS):
-                w_ap = w_huc[g][:, U + NB * j:U + NB * (j + 1)] if j < 2 else w_hc[:, j - 2, g, :]
-                mx_pass(acc_c[j], rq, g, w_ap, plane_h, 2 * U + NB * j, False, g == GROUPS - 1)
+        def hidden_pass(j, g):
+            c0, width = spans[j]
+            if j < 2:
+                w_ap = w_huc[g][:, U + c0:U + c0 + width]
+            else:
+                lo = c0 % NB
+                w_ap = w_hc[:, min(j - 2, 1), g, lo:lo + width]
+            mx_pass(acc_c[j][:, :width], rq, g, w_ap, plane_h, 2 * U + c0, False, g == GROUPS - 1)
 
         def add_bias(j):
+            c0, width = spans[j]
             z = work.tile([P, NB], F32, tag="z", name="z")
-            cand_sb[j] = work.tile([P, NB], F32, tag="cand", name="cand")
-            for h in range(2):
-                loc = slice(HALF * h, HALF * (h + 1))
-                c0 = 2 * U + NB * j + HALF * h
-                nc.vector.tensor_tensor(out=z[:, loc], in0=acc_c[j][:, loc], in1=bias_sb[:, c0:c0 + HALF], op=ADD)
-                nc.scalar.activation(out=cand_sb[j][:, loc], in_=z[:, loc], func=ACT.Tanh)
+            for a in range(0, width, HALF):
+                cols = slice(c0 + a, c0 + a + HALF)
+                nc.vector.tensor_tensor(
+                    out=z[:, a:a + HALF], in0=acc_c[j][:, a:a + HALF],
+                    in1=bias_sb[:, 2 * U + c0 + a:2 * U + c0 + a + HALF], op=ADD,
+                )
+                nc.scalar.activation(out=cand_sb[:, cols], in_=z[:, a:a + HALF], func=ACT.Tanh)
 
-        def multiply(j, h):
-            cols = slice(NB * j + HALF * h, NB * j + HALF * (h + 1))
-            nc.vector.tensor_tensor(out=out_sb[:, cols], in0=cand_sb[j][:, HALF * h:HALF * (h + 1)], in1=nu_sb[:, cols], op=MULT)
+        def multiply(h):
+            cols = slice(HALF * h, HALF * (h + 1))
+            nc.vector.tensor_tensor(out=out_sb[:, cols], in0=cand_sb[:, cols], in1=nu_sb[:, cols], op=MULT)
 
-        def finish(j, h):
-            cols = slice(NB * j + HALF * h, NB * j + HALF * (h + 1))
+        def finish(h):
+            cols = slice(HALF * h, HALF * (h + 1))
             nc.vector.tensor_tensor(out=out_sb[:, cols], in0=out_sb[:, cols], in1=uh_sb[:, cols], op=ADD)
 
-        def store(c0, c1):
-            nc.sync.dma_start(out=out[:, c0:c1], in_=out_sb[:, c0:c1])
+        def store(h0, h1):
+            cols = slice(HALF * h0, HALF * h1)
+            nc.sync.dma_start(out=out[:, cols], in_=out_sb[:, cols])
 
         with tc.manual_schedule(engines={mybir.EngineType.DVE}):
             input_passes(0)
-            hidden_passes(0)
-            hidden_passes(1)
             for j in (0, 1):
-                add_bias(j)
+                for g in range(GROUPS):
+                    hidden_pass(j, g)
+            add_bias(0)
+            add_bias(1)
             for step in (multiply, finish):
-                for j in (0, 1):
-                    step(j, 0)
-                    step(j, 1)
-            store(0, 2 * NB)
+                for h in range(4):
+                    step(h)
+            store(0, 4)
             input_passes(1)
-            hidden_passes(2)
+            for g in range(GROUPS):
+                hidden_pass(2, g)
             add_bias(2)
-            multiply(2, 0)
-            multiply(2, 1)
-            finish(2, 0)
-            hidden_passes(3)
+            multiply(4)
+            for j in (3, 4):
+                for g in range(GROUPS):
+                    hidden_pass(j, g)
             add_bias(3)
-            finish(2, 1)
-            store(2 * NB, 3 * NB)
-            multiply(3, 0)
-            multiply(3, 1)
-            for h in range(2):
-                finish(3, h)
-                store(3 * NB + HALF * h, 3 * NB + HALF * (h + 1))
+            multiply(5)
+            finish(4)
+            add_bias(4)
+            finish(5)
+            store(4, 6)
+            multiply(6)
+            multiply(7)
+            for h in (6, 7):
+                finish(h)
+                store(h, h + 1)

from contextlib import ExitStack

import concourse.mybir as mybir
from concourse.masks import make_identity

FLOPS = 2 * 128 * 2048 * (6144 + 4096 + 2048)

F32 = mybir.dt.float32
BF16 = mybir.dt.bfloat16
U8 = mybir.dt.uint8
U32 = mybir.dt.uint32
I32 = mybir.dt.int32
FP8X4 = mybir.dt.float8_e4m3fn_x4
ADD = mybir.AluOpType.add
MULT = mybir.AluOpType.mult
ACT = mybir.ActivationFunctionType

P = 128
U = 2048
NB = 512
GROUPS = 4


def tile_anothergrucell_w_kernel(tc, x_t, h_tm1, iw_words, iw_scales, hw_words, hw_scales, bias, out):
    nc = tc.nc
    with ExitStack() as ctx:
        const = ctx.enter_context(tc.tile_pool(name="const", bufs=1))
        wpool = ctx.enter_context(tc.tile_pool(name="wpool", bufs=4))
        work = ctx.enter_context(tc.tile_pool(name="work", bufs=2))
        psa = ctx.enter_context(tc.psum_pool(name="psa", bufs=1))
        psb = ctx.enter_context(tc.psum_pool(name="psb", bufs=4))

        plane_i = const.tile([P, 3 * U], U8, name="plane_i", align_bytes=64)
        plane_h = const.tile([P, 3 * U], U8, name="plane_h", align_bytes=64)
        nc.vector.memset(plane_i[:].bitcast(I32), 0)
        nc.vector.memset(plane_h[:].bitcast(I32), 0)
        bias_rows = const.tile([P, NB], BF16, name="bias_rows")
        nc.vector.memset(bias_rows[:], 0.0)
        warm_in = const.tile([P, 1], F32, name="warm_in")
        nc.vector.memset(warm_in[:], 0.0)
        warm_a = const.tile([P, 1], F32, name="warm_a")
        nc.scalar.activation(out=warm_a[:], in_=warm_in[:], func=ACT.Sigmoid)

        ident_f = const.tile([P, P], F32, name="ident_f")
        make_identity(nc, ident_f[:])
        ident_b = const.tile([P, P], BF16, name="ident_b")
        make_identity(nc, ident_b[:])

        x_sb = const.tile([P, U], BF16, tag="xr", name="x_sb")
        h_sb = const.tile([P, U], BF16, name="h_sb")
        nc.sync.dma_start(out=x_sb[:], in_=x_t)
        nc.scalar.dma_start(out=bias_rows[0:12, :], in_=bias.rearrange("(c n) -> c n", n=NB))
        for quads in ((2, 3), (0, 1)):
            for plane, scales in ((plane_i, iw_scales), (plane_h, hw_scales)):
                for q in quads:
                    nc.sync.dma_start(
                        out=plane[32 * q:32 * q + 16, :].bitcast(I32),
                        in_=scales[:, 4 * q:4 * q + 4, :].bitcast(I32),
                    )
        nc.sync.dma_start(out=h_sb[:], in_=h_tm1)

        def load(tile, words, g, c0, width):
            src = words[g].rearrange("p n t -> p (n t)")[:, 4 * c0:4 * (c0 + width)]
            nc.sync.dma_start(out=tile.bitcast(I32), in_=src.bitcast(I32))

        w_iru = []
        w_hr = []
        w_huc = []
        for g in range(GROUPS):
            w = wpool.tile([P, 2 * U], U32, tag="wide", name="w_iru", align_bytes=64)
            load(w[:], iw_words, g, 0, 2 * U)
            w_iru.append(w)
        for g in range(GROUPS):
            w = wpool.tile([P, U], U32, tag="reset", name="w_hr", align_bytes=64)
            load(w[:], hw_words, g, 0, U)
            w_hr.append(w)
        for g in range(GROUPS):
            w = wpool.tile([P, U + 2 * NB], U32, tag="update", name="w_huc", align_bytes=64)
            load(w[:], hw_words, g, U, U + 2 * NB)
            w_huc.append(w)

        def quantise(src_sb, banks, label):
            grp = work.tile([P, 4 * NB], BF16, tag="grp", name="grp_" + label, align_bytes=64)
            for b in range(2):
                tp = banks(b)
                for s in range(4):
                    g = 2 * b + s // 2
                    u = s % 2
                    nc.tensor.transpose(
                        tp[:, s, :],
                        src_sb[:].bitcast(F32)[:, 256 * g + u:256 * (g + 1):2],
                        ident_f[:],
                    )
                dst = grp[:].bitcast(F32)[:, NB * b:NB * (b + 1)].rearrange("p (a r u) -> p a r u", a=2, u=2)
                src = tp[:].rearrange("p (a u) r -> p a r u", u=2)
                if b == 0:
                    nc.vector.tensor_copy(out=dst, in_=src)
                else:
                    nc.scalar.copy(out=dst, in_=src)
            codes = const.tile([P, NB], U32, name="codes_" + label, align_bytes=64)
            scl = const.tile([P, NB], U8, name="scl_" + label, align_bytes=64)
            nc.vector.quantize_mx(out=codes[:].bitcast(FP8X4), scales=scl[:], in_=grp[:])
            return codes, scl

        def bank_b(label):
            def go(b):
                t = psb.tile([P, 4, P], F32, tag="b", name="tp_" + label)
                return t
            return go

        def bank_a(label):
            def go(b):
                t = psa.tile([P, 4, P], F32, tag="a%d" % b, name="tp_" + label)
                return t
            return go

        xq = quantise(x_sb, bank_b("x"), "x")
        hq = quantise(h_sb, bank_b("h"), "h")

        bias_sb = const.tile([P, 3 * U], BF16, name="bias_sb")
        for c in range(12):
            bp = psb.tile([P, NB], F32, tag="b", name="bp")
            nc.tensor.matmul(
                out=bp[:],
                lhsT=ident_b[:, c:c + 1].to_broadcast([P, P]),
                rhs=bias_rows[:],
                start=True,
                stop=True,
            )
            nc.scalar.copy(out=bias_sb[:, NB * c:NB * (c + 1)], in_=bp[:])

        def mx_pass(acc, act, g, w_ap, plane, c0, start, stop):
            codes, scl = act
            nc.tensor.matmul_mx(
                out=acc,
                lhsT=codes[:, P * g:P * (g + 1)].bitcast(FP8X4),
                lhsT_scale=scl[:, P * g:P * (g + 1)],
                rhs=w_ap.bitcast(FP8X4),
                rhs_scale=plane[4 * g:P, c0:c0 + w_ap.shape[1]],
                start=start,
                stop=stop,
            )

        acc_r = [psa.tile([P, NB], F32, tag="a%d" % j, name="acc_r%d" % j) for j in range(4)]
        acc_u = [psb.tile([P, NB], F32, tag="b", name="acc_u%d" % j) for j in range(4)]
        for g in range(GROUPS):
            for j, acc in enumerate(acc_r + acc_u):
                mx_pass(acc[:], xq, g, w_iru[g][:, NB * j:NB * (j + 1)], plane_i, NB * j, g == 0, False)

        w_ic = []
        for c0 in (2 * U, 2 * U + 2 * NB):
            w = wpool.tile([P, GROUPS, 2 * NB], U32, tag="wide", name="w_ic", align_bytes=64)
            for g in range(GROUPS):
                load(w[:, g, :], iw_words, g, c0, 2 * NB)
            w_ic.append(w)
        w_hc = wpool.tile([P, 2, GROUPS, NB], U32, tag="wide", name="w_hc", align_bytes=64)
        pieces = [(0, g, 0, NB) for g in range(GROUPS)] + [(1, 0, 0, NB)]
        pieces += [(1, g, a, NB // 2) for a in (0, NB // 2) for g in range(1, GROUPS)]
        for b, g, a, width in pieces:
            load(w_hc[:, b, g, a:a + width], hw_words, g, 2 * U + NB * (2 + b) + a, width)

        for g in range(GROUPS):
            for j in range(4):
                mx_pass(acc_r[j][:], hq, g, w_hr[g][:, NB * j:NB * (j + 1)], plane_h, NB * j, False, g == GROUPS - 1)
        rh_sb = const.tile([P, U], BF16, tag="xr", name="rh_sb")
        for j in range(4):
            cols = slice(NB * j, NB * (j + 1))
            z = work.tile([P, NB], F32, tag="z", name="z")
            nc.vector.tensor_tensor(out=z[:], in0=acc_r[j][:], in1=bias_sb[:, cols], op=ADD)
            r = work.tile([P, NB], F32, tag="r", name="r")
            nc.scalar.activation(out=r[:], in_=z[:], func=ACT.Sigmoid)
            nc.vector.tensor_tensor(out=rh_sb[:, cols], in0=r[:], in1=h_sb[:, cols], op=MULT)
        rq = quantise(rh_sb, bank_a("rh"), "rh")

        for g in range(GROUPS):
            for j in range(4):
                mx_pass(acc_u[j][:], hq, g, w_huc[g][:, NB * j:NB * (j + 1)], plane_h, U + NB * j, False, g == GROUPS - 1)
        uh_sb = const.tile([P, U], F32, name="uh_sb")
        nu_sb = const.tile([P, U], F32, name="nu_sb")
        for j in range(4):
            cols = slice(NB * j, NB * (j + 1))
            z = work.tile([P, NB], F32, tag="z", name="z")
            nc.vector.tensor_tensor(out=z[:], in0=acc_u[j][:], in1=bias_sb[:, U + NB * j:U + NB * (j + 1)], op=ADD)
            ug = work.tile([P, NB], F32, tag="r", name="ug")
            nc.scalar.activation(out=ug[:], in_=z[:], func=ACT.Sigmoid)
            nc.scalar.activation(out=nu_sb[:, cols], in_=z[:], func=ACT.Sigmoid, scale=-1.0)
            nc.vector.tensor_tensor(out=uh_sb[:, cols], in0=ug[:], in1=h_sb[:, cols], op=MULT)
        warm_b = const.tile([P, 1], F32, name="warm_b")
        nc.scalar.activation(out=warm_b[:], in_=nu_sb[:, U - 1:U], func=ACT.Tanh)

        HALF = NB // 2
        spans = [(0, NB), (NB, NB), (2 * NB, NB), (3 * NB, HALF), (3 * NB + HALF, HALF)]
        acc_c = [psa.tile([P, NB], F32, tag="a%d" % j, name="acc_c%d" % j) for j in range(4)]
        acc_c.append(psb.tile([P, NB], F32, tag="b", name="acc_c4"))
        out_sb = const.tile([P, U], F32, name="out_sb")
        cand_sb = const.tile([P, U], F32, name="cand_sb")

        def input_passes(b):
            for g in range(GROUPS):
                for acc, (c0, width) in zip(acc_c, spans):
                    lo = c0 - 2 * NB * b
                    if 0 <= lo < 2 * NB:
                        mx_pass(acc[:, :width], xq, g, w_ic[b][:, g, lo:lo + width], plane_i, 2 * U + c0, g == 0, False)

        def hidden_pass(j, g):
            c0, width = spans[j]
            if j < 2:
                w_ap = w_huc[g][:, U + c0:U + c0 + width]
            else:
                lo = c0 % NB
                w_ap = w_hc[:, min(j - 2, 1), g, lo:lo + width]
            mx_pass(acc_c[j][:, :width], rq, g, w_ap, plane_h, 2 * U + c0, False, g == GROUPS - 1)

        def add_bias(j):
            c0, width = spans[j]
            z = work.tile([P, NB], F32, tag="z", name="z")
            for a in range(0, width, HALF):
                cols = slice(c0 + a, c0 + a + HALF)
                nc.vector.tensor_tensor(
                    out=z[:, a:a + HALF], in0=acc_c[j][:, a:a + HALF],
                    in1=bias_sb[:, 2 * U + c0 + a:2 * U + c0 + a + HALF], op=ADD,
                )
                nc.scalar.activation(out=cand_sb[:, cols], in_=z[:, a:a + HALF], func=ACT.Tanh)

        def multiply(h):
            cols = slice(HALF * h, HALF * (h + 1))
            nc.vector.tensor_tensor(out=out_sb[:, cols], in0=cand_sb[:, cols], in1=nu_sb[:, cols], op=MULT)

        def finish(h):
            cols = slice(HALF * h, HALF * (h + 1))
            nc.vector.tensor_tensor(out=out_sb[:, cols], in0=out_sb[:, cols], in1=uh_sb[:, cols], op=ADD)

        def store(h0, h1):
            cols = slice(HALF * h0, HALF * h1)
            nc.sync.dma_start(out=out[:, cols], in_=out_sb[:, cols])

        with tc.manual_schedule(engines={mybir.EngineType.DVE}):
            input_passes(0)
            for j in (0, 1):
                for g in range(GROUPS):
                    hidden_pass(j, g)
            add_bias(0)
            add_bias(1)
            for step in (multiply, finish):
                for h in range(4):
                    step(h)
            store(0, 4)
            input_passes(1)
            for g in range(GROUPS):
                hidden_pass(2, g)
            add_bias(2)
            multiply(4)
            for j in (3, 4):
                for g in range(GROUPS):
                    hidden_pass(j, g)
            add_bias(3)
            multiply(5)
            finish(4)
            add_bias(4)
            finish(5)
            store(4, 6)
            multiply(6)
            multiply(7)
            for h in (6, 7):
                finish(h)
                store(h, h + 1)
